import numpy as np
import ml_dtypes


def mxq(x, axis, fmt="e4m3"):
    dtype, down = {"e4m3": (ml_dtypes.float8_e4m3fn, 7), "e5m2": (ml_dtypes.float8_e5m2, 14)}[fmt]
    v = np.moveaxis(np.asarray(x, np.float32).astype(ml_dtypes.bfloat16).astype(np.float64), axis, -1)
    blocks = v.reshape(v.shape[:-1] + (-1, 32))
    amax = np.abs(blocks).max(-1, keepdims=True)
    byte = np.maximum(np.where(amax > 0, np.frexp(amax)[1] - 1 + 127, 0) - down, 1)
    scale = np.exp2(byte - 127.0)
    codes = (blocks / scale).astype(np.float32).astype(dtype).astype(np.float64)
    return np.moveaxis((codes * scale).reshape(v.shape), -1, axis)


WIDE = False


def mx_kscale(k):
    if not WIDE:
        return np.ones(k)
    levels = np.array([18, -18])
    if k % 512:
        return np.exp2(np.random.permutation(np.resize(levels, k // 32))).repeat(32)
    a = np.empty((k // 512, 16))
    for p in range(k // 512):
        a[p, :8] = np.random.permutation(np.resize(levels, 8))
        for g in range(8):
            far = levels[np.abs(levels - a[p, g]) >= 10]
            a[p, g + 8] = far[np.random.randint(len(far))]
    return np.exp2(a.ravel()).repeat(32)


BF16 = ml_dtypes.bfloat16


def bf(x):
    return np.asarray(x, np.float32).astype(BF16)


def f64(x):
    return np.asarray(x).astype(np.float64)


B, C, H, W = 3, 512, 32, 32
T = B * H * W
BETA_MIN = 1e-06
REPARAM_OFFSET = 2.0 ** (-18)
PEDESTAL = REPARAM_OFFSET ** 2
BETA_BOUND = (BETA_MIN + PEDESTAL) ** 0.5
GAMMA_BOUND = REPARAM_OFFSET


def half_power(k):
    return np.exp2((np.frexp(k)[1] - 1) // 2)


def norm_of(inputs, beta, gamma):
    x2 = (f64(inputs) ** 2).reshape(B, C, H * W)
    beta_c = np.maximum(f64(beta), BETA_BOUND) ** 2 - PEDESTAL
    gamma_c = np.maximum(f64(gamma), GAMMA_BOUND) ** 2 - PEDESTAL
    return np.sqrt((gamma_c @ x2).reshape(B, C, H, W) + beta_c[None, :, None, None])


def setup_inputs():
    s = half_power(mx_kscale(T))
    s = (s / s.min()).reshape(B, 1, H, W)
    v = half_power(mx_kscale(C))
    amp = np.exp(0.5 * np.random.standard_normal((B, 1, H, W)))
    x0 = bf(2.0 * np.random.standard_normal((B, C, H, W)) * amp)
    beta = bf(0.5 + np.random.standard_normal(C))
    gamma0 = bf(np.random.standard_normal((C, C)) * 1.4 / np.sqrt(C))
    norm = norm_of(x0, beta, gamma0)
    vc = v[None, :, None, None]
    g = bf(4.0 * np.random.standard_normal((B, C, H, W)) * np.exp2(np.random.randint(-6, 1, (B, 1, H, W))) / s ** 3 * vc)
    return {"inputs": bf(f64(x0) * s * vc),
            "beta": beta,
            "gamma": bf(f64(gamma0) / v[:, None]),
            "norm": np.asarray(norm, np.float32),
            "grad_out": g}


def to_ct(a):
    return a.transpose(1, 0, 2, 3).reshape(C, T)


def reference(inputs, beta, gamma, norm, grad_out):
    x = to_ct(f64(inputs))
    n = to_ct(f64(norm))
    g = to_ct(f64(grad_out))
    gm = f64(gamma)
    gmax = np.maximum(gm, GAMMA_BOUND)
    gamma_c = gmax ** 2 - PEDESTAL
    x2 = x ** 2
    dn = -0.5 * g * x / n ** 3
    dx2 = mxq(gamma_c, 0, "e4m3").T @ mxq(dn, 0, "e5m2")
    dx = g / n + 2.0 * x * dx2
    dgamma_c = mxq(dn, 1, "e5m2") @ mxq(x2, 1, "e4m3").T
    dgamma = np.where(gm > GAMMA_BOUND, 2.0 * gmax * dgamma_c, 0.0)
    return dx.reshape(C, B, H, W).transpose(1, 0, 2, 3), dgamma

@@ -1,0 +1,332 @@
+from contextlib import ExitStack
+
+import concourse.mybir as mybir
+from concourse.masks import make_identity
+
+B, C, HW = 3, 512, 1024
+T = B * HW
+FLOPS = 2 * 2 * C * C * T
+
+F32 = mybir.dt.float32
+BF16 = mybir.dt.bfloat16
+U32 = mybir.dt.uint32
+U8 = mybir.dt.uint8
+E4 = mybir.dt.float8_e4m3fn_x4
+E5 = mybir.dt.float8_e5m2_x4
+ALU = mybir.AluOpType
+ACT = mybir.ActivationFunctionType
+
+P = 128
+J = 4
+G = 512
+NG = T // G
+GAMMA_BOUND = 2.0 ** (-18)
+PEDESTAL = 2.0 ** (-36)
+
+
+def tile_gdn_v_kernel(tc, inputs, beta, gamma, norm, grad_out, out_0, out_1):
+    nc = tc.nc
+    x_hbm = inputs.rearrange("b (p j) h w -> b p j (h w)", j=J)
+    g_hbm = grad_out.rearrange("b (p j) h w -> b p j (h w)", j=J)
+    n_hbm = norm.rearrange("b (p j) h w -> b p j (h w)", j=J)
+    o_hbm = out_0.rearrange("b (p j) h w -> b p j (h w)", j=J)
+
+    with ExitStack() as ctx:
+        keep = ctx.enter_context(tc.tile_pool(name="keep", bufs=1))
+        io = ctx.enter_context(tc.tile_pool(name="io", bufs=5))
+        work = ctx.enter_context(tc.tile_pool(name="work", bufs=2))
+        deep = ctx.enter_context(tc.tile_pool(name="deep", bufs=3))
+        codes_pool = ctx.enter_context(tc.tile_pool(name="codes", bufs=NG))
+        psum = ctx.enter_context(tc.psum_pool(name="psum", bufs=2))
+        accp = ctx.enter_context(tc.psum_pool(name="accp", bufs=1))
+        ctx.enter_context(tc.manual_schedule())
+
+        ident = keep.tile([P, P], F32, name="ident", align_bytes=64)
+        identb = keep.tile([P, P], BF16, name="identb", align_bytes=64)
+        warm = keep.tile([P, 8], F32, name="warm")
+        nc.vector.memset(warm[:], 1.0)
+        nc.scalar.activation(warm[:], warm[:], ACT.Abs_reciprocal_sqrt)
+
+        st = {}
+        ALLJ = slice(0, J)
+
+        def tok(i):
+            return i // 2, slice((i % 2) * G, (i % 2) * G + G)
+
+        def get(pool, tag, i, shape, dt):
+            if (tag, i) not in st:
+                new_tile = pool.tile(shape, dt, name=tag, align_bytes=64)
+                st[tag, i] = new_tile
+            return st[tag, i]
+
+        def dma_n(i, js=ALLJ):
+            b, w = tok(i)
+            n = get(deep, "n", i, [P, J, G], F32)
+            nc.sync.dma_start(out=n[:, js, :], in_=n_hbm[b, :, js, w])
+
+        def dma_g(i):
+            b, w = tok(i)
+            nc.sync.dma_start(out=get(io, "g", i, [P, J, G], BF16)[:], in_=g_hbm[b, :, :, w])
+
+        def dma_x(i):
+            b, w = tok(i)
+            nc.sync.dma_start(out=get(io, "x", i, [P, J, G], BF16)[:], in_=x_hbm[b, :, :, w])
+
+        def load(i):
+            dma_n(i)
+            dma_g(i)
+            dma_x(i)
+
+        def act_h(i, js=ALLJ):
+            h = get(work, "h", i, [P, J, G], F32)
+            nc.scalar.activation(h[:, js, :], st["n", i][:, js, :], ACT.Abs_reciprocal_sqrt)
+
+        def act_r(i, js=ALLJ):
+            r = get(work, "r", i, [P, J, G], F32)
+            nc.scalar.activation(r[:, js, :], st["h", i][:, js, :], ACT.Square)
+
+        def act_r2(i, js=ALLJ):
+            nc.scalar.activation(st["h", i][:, js, :], st["r", i][:, js, :], ACT.Square)
+
+        def make_e(engine, i, js=ALLJ):
+            e = get(keep, "e", i, [P, J, G], F32)
+            engine.tensor_tensor(out=e[:, js, :], in0=st["n", i][:, js, :], in1=st["r", i][:, js, :], op=ALU.mult)
+
+        def vec_a(i, js=ALLJ):
+            a = get(deep, "a", i, [P, J, G], F32)
+            nc.vector.tensor_tensor(out=a[:, js, :], in0=st["g", i][:, js, :], in1=st["r", i][:, js, :], op=ALU.mult)
+
+        def vec_w(i, js=ALLJ):
+            e = st["e", i]
+            nc.vector.scalar_tensor_tensor(out=e[:, js, :], in0=e[:, js, :], scalar=4.0 / 3.0, in1=st["a", i][:, js, :], op0=ALU.subtract, op1=ALU.mult)
+
+        def pe_x(i):
+            for half in range(2):
+                xp = psum.tile([P, 2 * G], BF16, name="xp")
+                st["xp", i, half] = xp
+                for jj in range(2):
+                    nc.tensor.matmul(xp[:, jj * G : jj * G + G], lhsT=identb[:], rhs=st["x", i][:, 2 * half + jj, :], start=True, stop=True)
+
+        def vec_t(i, from_psum):
+            t = get(keep, "t", i, [P, J, G], F32)
+            if from_psum:
+                for half in range(2):
+                    js = slice(2 * half, 2 * half + 2)
+                    nc.vector.tensor_tensor(
+                        out=t[:, js, :].rearrange("p j w -> p (j w)"),
+                        in0=st["xp", i, half][:],
+                        in1=st["h", i][:, js, :].rearrange("p j w -> p (j w)"),
+                        op=ALU.mult,
+                    )
+            else:
+                nc.vector.tensor_tensor(out=t[:], in0=st["x", i][:], in1=st["h", i][:], op=ALU.mult)
+
+        def vec_dn(i):
+            dn = get(work, "dn", i, [P, J, G], BF16)
+            nc.vector.scalar_tensor_tensor(out=dn[:], in0=st["e", i][:], scalar=1.5, in1=st["t", i][:], op0=ALU.mult, op1=ALU.mult)
+
+        def pe_turn(i, key):
+            words = st[key, i][:].rearrange("p j w -> p (j w)").bitcast(F32)
+            for hb in range(2):
+                tp = psum.tile([P, 2, 2 * P], F32, name="tp")
+                st["turned", key, i, hb] = tp
+                for u in range(2):
+                    for jj in range(2):
+                        j = 2 * hb + jj
+                        nc.tensor.transpose(tp[:, u, jj * P : jj * P + P], words[:, j * (G // 2) + u : (j + 1) * (G // 2) : 2], ident[:])
+
+        def act_x2(i):
+            x2 = get(work, "x2", i, [P, 4 * C], BF16)
+            for hb in range(2):
+                tp = st["turned", "x", i, hb]
+                nc.scalar.activation(
+                    x2[:, 1024 * hb : 1024 * hb + 1024].rearrange("q (c u e) -> q c u e", u=2, e=2),
+                    tp[:].rearrange("q u c -> q (u c)").bitcast(BF16).rearrange("q (u c e) -> q c u e", u=2, e=2),
+                    ACT.Square,
+                )
+
+        def act_dt(i):
+            dt = get(work, "dt", i, [P, 4 * C], BF16)
+            for hb in range(2):
+                tp = st["turned", "dn", i, hb]
+                nc.scalar.copy(
+                    dt[:].bitcast(F32)[:, 512 * hb : 512 * hb + 512].rearrange("q (c u) -> q c u", u=2),
+                    tp[:].rearrange("q u c -> q c u"),
+                )
+
+        def copy_di(copy, i, ws=slice(0, G)):
+            di = get(work, "di", i, [P, G, J], BF16)
+            copy(di[:, ws, :], st["dn", i][:, :, ws].rearrange("p j w -> p w j"))
+
+        def quant(key, pool, i, dt):
+            codes = get(pool, key + "q", i, [P, G], U32)
+            scales = get(pool, key + "s", i, [P, G], U8)
+            src = st[key, i][:]
+            if key == "di":
+                src = src.rearrange("p w j -> p (w j)")
+            nc.vector.quantize_mx(out=codes[:].bitcast(dt), scales=scales[:], in_=src)
+
+        def pe_mm0(i, tiles):
+            for t in tiles:
+                pp = psum.tile([P, G], F32, name="pp")
+                st["pp", i, t] = pp
+                cols = slice(P * t, P * t + P)
+                nc.tensor.matmul_mx(
+                    out=pp[:], lhsT=gq[:, cols].bitcast(E4), lhsT_scale=gs[:, cols],
+                    rhs=st["diq", i][:].bitcast(E5), rhs_scale=st["dis", i][:], start=True, stop=True,
+                )
+
+        def pe_mm1(i, tiles):
+            for j in tiles:
+                cols = slice(P * j, P * j + P)
+                nc.tensor.matmul_mx(
+                    out=acc[j][:], lhsT=st["dtq", i][:, cols].bitcast(E5), lhsT_scale=st["dts", i][:, cols],
+                    rhs=st["x2q", i][:].bitcast(E4), rhs_scale=st["x2s", i][:], start=(i == 0), stop=(i == NG - 1),
+                )
+
+        def vec_u(i, t):
+            u = get(work, "u", i, [P, J, G], F32)
+            nc.vector.scalar_tensor_tensor(out=u[:, t, :], in0=st["pp", i, t][:], scalar=2.0, in1=st["x", i][:, t, :], op0=ALU.mult, op1=ALU.mult)
+
+        def add_o(engine, i, js=ALLJ):
+            u = st["u", i]
+            engine.tensor_tensor(out=u[:, js, :], in0=u[:, js, :], in1=st["a", i][:, js, :], op=ALU.add)
+
+        def store(i, js=ALLJ):
+            b, w = tok(i)
+            nc.sync.dma_start(out=o_hbm[b, :, js, w], in_=st["u", i][:, js, :])
+
+        acc = []
+        for j in range(2):
+            acc_j = accp.tile([P, C], F32, name="acc%d" % j)
+            acc.append(acc_j)
+
+        lo, hi = slice(0, 2), slice(2, 4)
+        gam = keep.tile([P, J, C], BF16, name="gam", align_bytes=64)
+        nc.sync.dma_start(out=gam[:], in_=gamma.rearrange("(p j) c -> p j c", j=J))
+        dma_n(0, lo)
+        dma_g(0)
+        dma_n(0, hi)
+        dma_x(0)
+        load(1)
+        load(2)
+        make_identity(nc, ident[:])
+        make_identity(nc, identb[:])
+
+        gm = work.tile([P, J, C], BF16, name="dn", align_bytes=64)
+        nc.vector.tensor_scalar_max(gm[:], gam[:], GAMMA_BOUND)
+        sq = keep.tile([P, J, G], F32, name="t", align_bytes=64)
+        nc.vector.tensor_tensor(out=sq[:], in0=gm[:], in1=gm[:], op=ALU.mult)
+        gi = work.tile([P, C * J], BF16, name="di", align_bytes=64)
+        gq = keep.tile([P, C], U32, name="gq", align_bytes=64)
+        gs = keep.tile([P, C], U8, name="gs", align_bytes=64)
+        nc.vector.tensor_scalar_add(
+            gi[:].rearrange("p (t m j) -> p t m j", t=4, j=J),
+            sq[:].rearrange("p j (m t) -> p t m j", t=4),
+            -PEDESTAL,
+        )
+        coef = keep.tile([P, J, C], BF16, name="coef", align_bytes=64)
+        nc.gpsimd.tensor_scalar(coef[:], gam[:], GAMMA_BOUND, 1.0, op0=ALU.is_gt, op1=ALU.mult)
+        nc.gpsimd.tensor_tensor(out=coef[:], in0=coef[:], in1=gam[:], op=ALU.mult)
+
+        for js in (lo, hi):
+            act_h(0, js)
+            act_r(0, js)
+        act_r2(0)
+        pe_turn(0, "x")
+        act_h(1)
+        act_r(1)
+        act_x2(0)
+        act_r2(1)
+        for js in (lo, hi):
+            vec_a(0, js)
+            make_e(nc.vector, 0, js)
+        vec_t(0, False)
+        vec_w(0)
+        nc.vector.quantize_mx(out=gq[:].bitcast(E4), scales=gs[:], in_=gi[:])
+        vec_dn(0)
+        make_e(nc.gpsimd, 1)
+        copy_di(nc.scalar.copy, 0)
+        pe_turn(0, "dn")
+        act_dt(0)
+        pe_turn(1, "x")
+        act_x2(1)
+        act_h(2)
+        act_r(2)
+        act_r2(2)
+        vec_t(1, False)
+        vec_a(1)
+        quant("x2", codes_pool, 0, E4)
+        quant("di", work, 0, E5)
+        quant("dt", codes_pool, 0, E5)
+        pe_mm0(0, (0, 1))
+        pe_mm1(0, (0, 1))
+
+        for i in range(NG - 1):
+            if i + 3 < NG:
+                load(i + 3)
+            vec_w(i + 1)
+            if i > 0:
+                add_o(nc.vector, i - 1)
+                store(i - 1)
+            if i + 2 < NG:
+                pe_x(i + 2)
+                pe_turn(i + 2, "x")
+                act_x2(i + 2)
+            vec_dn(i + 1)
+            pe_turn(i + 1, "dn")
+            copy_di(nc.scalar.copy, i + 1)
+            act_dt(i + 1)
+            if i + 2 < NG:
+                for js in (lo, hi):
+                    make_e(nc.gpsimd, i + 2, js)
+                vec_t(i + 2, True)
+            if i + 3 < NG:
+                act_h(i + 3)
+                act_r(i + 3)
+                act_r2(i + 3)
+            pe_mm0(i, (2, 3))
+            for t in range(J):
+                vec_u(i, t)
+            if i + 2 < NG:
+                vec_a(i + 2)
+            quant("x2", codes_pool, i + 1, E4)
+            quant("di", work, i + 1, E5)
+            quant("dt", codes_pool, i + 1, E5)
+            pe_mm0(i + 1, (0, 1))
+            pe_mm1(i + 1, (0, 1))
+
+        for j in (2, 3):
+            acc_j = psum.tile([P, C], F32, name="tp")
+            acc.append(acc_j)
+        last = NG - 1
+        o1 = keep.tile([P, J, C], F32, name="t", align_bytes=64)
+
+        def vec_o1(j):
+            nc.vector.scalar_tensor_tensor(
+                out=o1[:, j, :].rearrange("p (q k) -> p q k", k=J),
+                in0=acc[j][:].rearrange("p (k q) -> p q k", k=J),
+                scalar=2.0,
+                in1=coef[:, j, :].rearrange("p (q k) -> p q k", k=J),
+                op0=ALU.mult, op1=ALU.mult,
+            )
+
+        o1_hbm = out_1.rearrange("(p j) c -> p j c", j=J)
+        add_o(nc.vector, last - 1)
+        store(last - 1)
+        pe_mm0(last, (2, 3))
+        for i in range(NG):
+            pe_mm1(i, (2, 3))
+        vec_u(last, 0)
+        vec_u(last, 1)
+        add_o(nc.gpsimd, last, slice(0, 1))
+        store(last, slice(0, 1))
+        vec_u(last, 2)
+        vec_u(last, 3)
+        add_o(nc.vector, last, slice(1, 4))
+        store(last, slice(1, 4))
+        for half in range(2):
+            vec_o1(2 * half)
+            vec_o1(2 * half + 1)
+            js = slice(2 * half, 2 * half + 2)
+            nc.sync.dma_start(out=o1_hbm[:, js, :], in_=o1[:, js, :])

@@ -22,6 +22,38 @@ G = 512
 NG = T // G
 GAMMA_BOUND = 2.0 ** (-18)
 PEDESTAL = 2.0 ** (-36)
+FINE = (0,)
+NEWTON = (0,)
+DN_BUFS = (4, 2, 2, 5)
+LOADS = ("gam", "n")
+ORDER = (
+    ("coef", 5),
+    ("gsq", 3),
+    ("q_dt", -2),
+    ("q_dn", 1),
+    ("ub", 0),
+    ("turn_dn", 0),
+    ("a", 2),
+    ("mm0a", 1),
+    ("load", 4),
+    ("gi", 2),
+    ("w", 2),
+    ("t", 2),
+    ("gq", 2),
+    ("first", 4),
+    ("dt", 0),
+    ("mm1", -3),
+    ("second", 3),
+    ("ua", 1),
+    ("turn_x", 0),
+    ("o", 0),
+    ("third", 3),
+    ("mm0b", 1),
+    ("x2", 0),
+    ("q_x2", -1),
+    ("dn", 2),
+    ("p", 4),
+)
 
 
 def tile_gdn_v_kernel(tc, inputs, beta, gamma, norm, grad_out, out_0, out_1):
@@ -33,22 +65,26 @@ def tile_gdn_v_kernel(tc, inputs, beta, gamma, norm, grad_out, out_0, out_1):
 
     with ExitStack() as ctx:
         keep = ctx.enter_context(tc.tile_pool(name="keep", bufs=1))
-        io = ctx.enter_context(tc.tile_pool(name="io", bufs=5))
         work = ctx.enter_context(tc.tile_pool(name="work", bufs=2))
         deep = ctx.enter_context(tc.tile_pool(name="deep", bufs=3))
-        codes_pool = ctx.enter_context(tc.tile_pool(name="codes", bufs=NG))
+        io = ctx.enter_context(tc.tile_pool(name="io", bufs=DN_BUFS[3]))
+        dnp = ctx.enter_context(tc.tile_pool(name="dnp", bufs=DN_BUFS[0]))
+        up = ctx.enter_context(tc.tile_pool(name="up", bufs=DN_BUFS[1]))
+        tpl = ctx.enter_context(tc.tile_pool(name="tpl", bufs=DN_BUFS[2]))
+        whole = ctx.enter_context(tc.tile_pool(name="whole", bufs=NG))
         psum = ctx.enter_context(tc.psum_pool(name="psum", bufs=2))
         accp = ctx.enter_context(tc.psum_pool(name="accp", bufs=1))
-        ctx.enter_context(tc.manual_schedule())
+
+        lo, hi = slice(0, 2), slice(2, 4)
+        ALLJ = (slice(0, J),)
+        HALVES = (lo, hi)
 
         ident = keep.tile([P, P], F32, name="ident", align_bytes=64)
-        identb = keep.tile([P, P], BF16, name="identb", align_bytes=64)
         warm = keep.tile([P, 8], F32, name="warm")
         nc.vector.memset(warm[:], 1.0)
         nc.scalar.activation(warm[:], warm[:], ACT.Abs_reciprocal_sqrt)
 
         st = {}
-        ALLJ = slice(0, J)
 
         def tok(i):
             return i // 2, slice((i % 2) * G, (i % 2) * G + G)
@@ -59,86 +95,101 @@ def tile_gdn_v_kernel(tc, inputs, beta, gamma, norm, grad_out, out_0, out_1):
                 st[tag, i] = new_tile
             return st[tag, i]
 
-        def dma_n(i, js=ALLJ):
-            b, w = tok(i)
-            n = get(deep, "n", i, [P, J, G], F32)
-            nc.sync.dma_start(out=n[:, js, :], in_=n_hbm[b, :, js, w])
+        def first_parts(i):
+            return HALVES if i in FINE else ALLJ
 
-        def dma_g(i):
+        def load_n(i):
+            b, w = tok(i)
+            n = get(io, "n", i, [P, J, G], F32)
+            for js in first_parts(i):
+                nc.sync.dma_start(out=n[:, js, :], in_=n_hbm[b, :, js, w])
+
+        def load_g(i):
             b, w = tok(i)
             nc.sync.dma_start(out=get(io, "g", i, [P, J, G], BF16)[:], in_=g_hbm[b, :, :, w])
 
-        def dma_x(i):
+        def load_x(i):
             b, w = tok(i)
-            nc.sync.dma_start(out=get(io, "x", i, [P, J, G], BF16)[:], in_=x_hbm[b, :, :, w])
+            nc.sync.dma_start(out=get(whole, "x", i, [P, J, G], BF16)[:], in_=x_hbm[b, :, :, w])
 
         def load(i):
-            dma_n(i)
-            dma_g(i)
-            dma_x(i)
+            load_n(i)
+            load_g(i)
+            load_x(i)
 
-        def act_h(i, js=ALLJ):
-            h = get(work, "h", i, [P, J, G], F32)
-            nc.scalar.activation(h[:, js, :], st["n", i][:, js, :], ACT.Abs_reciprocal_sqrt)
+        def act_first(i):
+            n, b = st["n", i], get(deep, "b", i, [P, J, G], F32)
+            for js in first_parts(i):
+                if i in NEWTON:
+                    a = get(deep, "a", i, [P, J, G], F32)
+                    nc.scalar.activation(b[:, js, :], n[:, js, :], ACT.Abs_reciprocal_sqrt)
+                    nc.scalar.activation(a[:, js, :], b[:, js, :], ACT.Square)
+                else:
+                    nc.scalar.activation(n[:, js, :], n[:, js, :], ACT.Square)
+                    nc.scalar.activation(b[:, js, :], n[:, js, :], ACT.Abs_reciprocal_sqrt)
 
-        def act_r(i, js=ALLJ):
-            r = get(work, "r", i, [P, J, G], F32)
-            nc.scalar.activation(r[:, js, :], st["h", i][:, js, :], ACT.Square)
+        def vec_p(i):
+            n = st["n", i]
+            for js in first_parts(i):
+                nc.vector.tensor_tensor(out=n[:, js, :], in0=n[:, js, :], in1=st["a" if i in NEWTON else "b", i][:, js, :], op=ALU.mult)
 
-        def act_r2(i, js=ALLJ):
-            nc.scalar.activation(st["h", i][:, js, :], st["r", i][:, js, :], ACT.Square)
+        def act_second(i):
+            n = st["n", i]
+            for js in () if i in NEWTON else first_parts(i):
+                nc.scalar.activation(n[:, js, :], n[:, js, :], ACT.Square)
+                nc.scalar.activation(n[:, js, :], n[:, js, :], ACT.Abs_reciprocal_sqrt)
 
-        def make_e(engine, i, js=ALLJ):
-            e = get(keep, "e", i, [P, J, G], F32)
-            engine.tensor_tensor(out=e[:, js, :], in0=st["n", i][:, js, :], in1=st["r", i][:, js, :], op=ALU.mult)
+        def vec_w(i):
+            n = st["n", i]
+            for js in first_parts(i) if i in NEWTON else ():
+                nc.vector.scalar_tensor_tensor(out=n[:, js, :], in0=n[:, js, :], scalar=4.0 / 3.0, in1=st["a", i][:, js, :], op0=ALU.subtract, op1=ALU.mult)
 
-        def vec_a(i, js=ALLJ):
+        def act_third(i):
+            n, b = st["n", i], st["b", i]
+            for js in first_parts(i):
+                r = st["a", i] if i in NEWTON else n
+                nc.scalar.activation(b[:, js, :], r[:, js, :], ACT.Square)
+
+        def vec_a(i):
             a = get(deep, "a", i, [P, J, G], F32)
-            nc.vector.tensor_tensor(out=a[:, js, :], in0=st["g", i][:, js, :], in1=st["r", i][:, js, :], op=ALU.mult)
+            r = a if i in NEWTON else st["n", i]
+            for js in first_parts(i):
+                nc.vector.tensor_tensor(out=a[:, js, :], in0=st["g", i][:, js, :], in1=r[:, js, :], op=ALU.mult)
 
-        def vec_w(i, js=ALLJ):
-            e = st["e", i]
-            nc.vector.scalar_tensor_tensor(out=e[:, js, :], in0=e[:, js, :], scalar=4.0 / 3.0, in1=st["a", i][:, js, :], op0=ALU.subtract, op1=ALU.mult)
-
-        def pe_x(i):
-            for half in range(2):
-                xp = psum.tile([P, 2 * G], BF16, name="xp")
-                st["xp", i, half] = xp
-                for jj in range(2):
-                    nc.tensor.matmul(xp[:, jj * G : jj * G + G], lhsT=identb[:], rhs=st["x", i][:, 2 * half + jj, :], start=True, stop=True)
-
-        def vec_t(i, from_psum):
-            t = get(keep, "t", i, [P, J, G], F32)
-            if from_psum:
-                for half in range(2):
-                    js = slice(2 * half, 2 * half + 2)
-                    nc.vector.tensor_tensor(
-                        out=t[:, js, :].rearrange("p j w -> p (j w)"),
-                        in0=st["xp", i, half][:],
-                        in1=st["h", i][:, js, :].rearrange("p j w -> p (j w)"),
-                        op=ALU.mult,
-                    )
-            else:
-                nc.vector.tensor_tensor(out=t[:], in0=st["x", i][:], in1=st["h", i][:], op=ALU.mult)
+        def vec_t(i):
+            t = get(tpl, "t", i, [P, J, G], F32)
+            for js in first_parts(i):
+                nc.vector.tensor_tensor(out=t[:, js, :], in0=st["x", i][:, js, :], in1=st["b", i][:, js, :], op=ALU.mult)
 
         def vec_dn(i):
-            dn = get(work, "dn", i, [P, J, G], BF16)
-            nc.vector.scalar_tensor_tensor(out=dn[:], in0=st["e", i][:], scalar=1.5, in1=st["t", i][:], op0=ALU.mult, op1=ALU.mult)
+            dn = get(dnp, "dn", i, [P, G, J], BF16)
+            nc.vector.scalar_tensor_tensor(
+                out=dn[:], in0=st["n" if i in NEWTON else "a", i][:].rearrange("p j w -> p w j"), scalar=1.5 if i in NEWTON else -0.5,
+                in1=st["t", i][:].rearrange("p j w -> p w j"), op0=ALU.mult, op1=ALU.mult,
+            )
 
-        def pe_turn(i, key):
-            words = st[key, i][:].rearrange("p j w -> p (j w)").bitcast(F32)
+        def pe_turn_x(i):
+            words = st["x", i][:].rearrange("p j w -> p (j w)").bitcast(F32)
             for hb in range(2):
                 tp = psum.tile([P, 2, 2 * P], F32, name="tp")
-                st["turned", key, i, hb] = tp
+                st["xt", i, hb] = tp
                 for u in range(2):
                     for jj in range(2):
                         j = 2 * hb + jj
                         nc.tensor.transpose(tp[:, u, jj * P : jj * P + P], words[:, j * (G // 2) + u : (j + 1) * (G // 2) : 2], ident[:])
 
+        def pe_turn_dn(i):
+            words = st["dn", i][:].rearrange("p w j -> p (w j)").bitcast(F32)
+            for hb in range(2):
+                tp = psum.tile([P, J, P], F32, name="tp")
+                st["dt", i, hb] = tp
+                for t in range(4):
+                    nc.tensor.transpose(tp[:, t, :], words[:, 2 * t + hb : 2 * G : 8], ident[:])
+
         def act_x2(i):
             x2 = get(work, "x2", i, [P, 4 * C], BF16)
             for hb in range(2):
-                tp = st["turned", "x", i, hb]
+                tp = st["xt", i, hb]
                 nc.scalar.activation(
                     x2[:, 1024 * hb : 1024 * hb + 1024].rearrange("q (c u e) -> q c u e", u=2, e=2),
                     tp[:].rearrange("q u c -> q (u c)").bitcast(BF16).rearrange("q (u c e) -> q c u e", u=2, e=2),
@@ -146,25 +197,29 @@ def tile_gdn_v_kernel(tc, inputs, beta, gamma, norm, grad_out, out_0, out_1):
                 )
 
         def act_dt(i):
-            dt = get(work, "dt", i, [P, 4 * C], BF16)
+            dt = get(work, "dtt", i, [P, 4 * C], BF16)
             for hb in range(2):
-                tp = st["turned", "dn", i, hb]
                 nc.scalar.copy(
-                    dt[:].bitcast(F32)[:, 512 * hb : 512 * hb + 512].rearrange("q (c u) -> q c u", u=2),
-                    tp[:].rearrange("q u c -> q c u"),
+                    dt[:, 1024 * hb : 1024 * hb + 1024].rearrange("q (b m t) -> q b m t", b=2, t=4),
+                    st["dt", i, hb][:].rearrange("q t m -> q (t m)").bitcast(BF16).rearrange("q (t m b) -> q b m t", t=4, b=2),
                 )
-
-        def copy_di(copy, i, ws=slice(0, G)):
-            di = get(work, "di", i, [P, G, J], BF16)
-            copy(di[:, ws, :], st["dn", i][:, :, ws].rearrange("p j w -> p w j"))
 
         def quant(key, pool, i, dt):
             codes = get(pool, key + "q", i, [P, G], U32)
             scales = get(pool, key + "s", i, [P, G], U8)
             src = st[key, i][:]
-            if key == "di":
+            if key == "dn":
                 src = src.rearrange("p w j -> p (w j)")
             nc.vector.quantize_mx(out=codes[:].bitcast(dt), scales=scales[:], in_=src)
+
+        def q_dn(i):
+            quant("dn", work, i, E5)
+
+        def q_dt(i):
+            quant("dtt", work, i, E5)
+
+        def q_x2(i):
+            quant("x2", work, i, E4)
 
         def pe_mm0(i, tiles):
             for t in tiles:
@@ -173,160 +228,109 @@ def tile_gdn_v_kernel(tc, inputs, beta, gamma, norm, grad_out, out_0, out_1):
                 cols = slice(P * t, P * t + P)
                 nc.tensor.matmul_mx(
                     out=pp[:], lhsT=gq[:, cols].bitcast(E4), lhsT_scale=gs[:, cols],
-                    rhs=st["diq", i][:].bitcast(E5), rhs_scale=st["dis", i][:], start=True, stop=True,
+                    rhs=st["dnq", i][:].bitcast(E5), rhs_scale=st["dns", i][:], start=True, stop=True,
                 )
 
-        def pe_mm1(i, tiles):
-            for j in tiles:
+        def pe_mm0a(i):
+            pe_mm0(i, (0, 1))
+
+        def pe_mm0b(i):
+            pe_mm0(i, (2, 3))
+
+        def pe_mm1(i):
+            for j in range(J):
                 cols = slice(P * j, P * j + P)
                 nc.tensor.matmul_mx(
-                    out=acc[j][:], lhsT=st["dtq", i][:, cols].bitcast(E5), lhsT_scale=st["dts", i][:, cols],
+                    out=acc[j][:], lhsT=st["dttq", i][:, cols].bitcast(E5), lhsT_scale=st["dtts", i][:, cols],
                     rhs=st["x2q", i][:].bitcast(E4), rhs_scale=st["x2s", i][:], start=(i == 0), stop=(i == NG - 1),
                 )
 
-        def vec_u(i, t):
-            u = get(work, "u", i, [P, J, G], F32)
-            nc.vector.scalar_tensor_tensor(out=u[:, t, :], in0=st["pp", i, t][:], scalar=2.0, in1=st["x", i][:, t, :], op0=ALU.mult, op1=ALU.mult)
+        def vec_u(i, tiles):
+            u = get(up, "u", i, [P, J, G], F32)
+            for t in tiles:
+                nc.vector.scalar_tensor_tensor(out=u[:, t, :], in0=st["x", i][:, t, :], scalar=2.0, in1=st["pp", i, t][:], op0=ALU.mult, op1=ALU.mult)
 
-        def add_o(engine, i, js=ALLJ):
-            u = st["u", i]
-            engine.tensor_tensor(out=u[:, js, :], in0=u[:, js, :], in1=st["a", i][:, js, :], op=ALU.add)
+        def vec_ua(i):
+            vec_u(i, (0, 1))
 
-        def store(i, js=ALLJ):
+        def vec_ub(i):
+            vec_u(i, (2, 3))
+
+        def vec_o(i):
             b, w = tok(i)
-            nc.sync.dma_start(out=o_hbm[b, :, js, w], in_=st["u", i][:, js, :])
+            u = st["u", i]
+            for js in HALVES if i == NG - 1 else ALLJ:
+                nc.vector.tensor_tensor(out=u[:, js, :], in0=u[:, js, :], in1=st["a", i][:, js, :], op=ALU.add)
+                nc.sync.dma_start(out=o_hbm[b, :, js, w], in_=u[:, js, :])
 
         acc = []
-        for j in range(2):
+        for j in range(J):
             acc_j = accp.tile([P, C], F32, name="acc%d" % j)
             acc.append(acc_j)
 
-        lo, hi = slice(0, 2), slice(2, 4)
         gam = keep.tile([P, J, C], BF16, name="gam", align_bytes=64)
-        nc.sync.dma_start(out=gam[:], in_=gamma.rearrange("(p j) c -> p j c", j=J))
-        dma_n(0, lo)
-        dma_g(0)
-        dma_n(0, hi)
-        dma_x(0)
-        load(1)
-        load(2)
+        for what in LOADS:
+            if what == "gam":
+                nc.sync.dma_start(out=gam[:], in_=gamma.rearrange("(p j) c -> p j c", j=J))
+            if what == "n":
+                load_n(0)
+        load_g(0)
+        load_x(0)
+        for i in range(1, 4):
+            load(i)
         make_identity(nc, ident[:])
-        make_identity(nc, identb[:])
 
-        gm = work.tile([P, J, C], BF16, name="dn", align_bytes=64)
+        gm = work.tile([P, J, C], BF16, name="x2", align_bytes=64)
         nc.vector.tensor_scalar_max(gm[:], gam[:], GAMMA_BOUND)
-        sq = keep.tile([P, J, G], F32, name="t", align_bytes=64)
-        nc.vector.tensor_tensor(out=sq[:], in0=gm[:], in1=gm[:], op=ALU.mult)
-        gi = work.tile([P, C * J], BF16, name="di", align_bytes=64)
+        sq = deep.tile([P, J, G], F32, name="b", align_bytes=64)
+        gi = work.tile([P, C * J], BF16, name="dtt", align_bytes=64)
         gq = keep.tile([P, C], U32, name="gq", align_bytes=64)
         gs = keep.tile([P, C], U8, name="gs", align_bytes=64)
-        nc.vector.tensor_scalar_add(
-            gi[:].rearrange("p (t m j) -> p t m j", t=4, j=J),
-            sq[:].rearrange("p j (m t) -> p t m j", t=4),
-            -PEDESTAL,
-        )
         coef = keep.tile([P, J, C], BF16, name="coef", align_bytes=64)
-        nc.gpsimd.tensor_scalar(coef[:], gam[:], GAMMA_BOUND, 1.0, op0=ALU.is_gt, op1=ALU.mult)
-        nc.gpsimd.tensor_tensor(out=coef[:], in0=coef[:], in1=gam[:], op=ALU.mult)
 
-        for js in (lo, hi):
-            act_h(0, js)
-            act_r(0, js)
-        act_r2(0)
-        pe_turn(0, "x")
-        act_h(1)
-        act_r(1)
-        act_x2(0)
-        act_r2(1)
-        for js in (lo, hi):
-            vec_a(0, js)
-            make_e(nc.vector, 0, js)
-        vec_t(0, False)
-        vec_w(0)
-        nc.vector.quantize_mx(out=gq[:].bitcast(E4), scales=gs[:], in_=gi[:])
-        vec_dn(0)
-        make_e(nc.gpsimd, 1)
-        copy_di(nc.scalar.copy, 0)
-        pe_turn(0, "dn")
-        act_dt(0)
-        pe_turn(1, "x")
-        act_x2(1)
-        act_h(2)
-        act_r(2)
-        act_r2(2)
-        vec_t(1, False)
-        vec_a(1)
-        quant("x2", codes_pool, 0, E4)
-        quant("di", work, 0, E5)
-        quant("dt", codes_pool, 0, E5)
-        pe_mm0(0, (0, 1))
-        pe_mm1(0, (0, 1))
+        def gamma_sq(i):
+            if i == 0:
+                nc.scalar.activation(sq[:], gm[:], ACT.Square)
 
-        for i in range(NG - 1):
-            if i + 3 < NG:
-                load(i + 3)
-            vec_w(i + 1)
-            if i > 0:
-                add_o(nc.vector, i - 1)
-                store(i - 1)
-            if i + 2 < NG:
-                pe_x(i + 2)
-                pe_turn(i + 2, "x")
-                act_x2(i + 2)
-            vec_dn(i + 1)
-            pe_turn(i + 1, "dn")
-            copy_di(nc.scalar.copy, i + 1)
-            act_dt(i + 1)
-            if i + 2 < NG:
-                for js in (lo, hi):
-                    make_e(nc.gpsimd, i + 2, js)
-                vec_t(i + 2, True)
-            if i + 3 < NG:
-                act_h(i + 3)
-                act_r(i + 3)
-                act_r2(i + 3)
-            pe_mm0(i, (2, 3))
-            for t in range(J):
-                vec_u(i, t)
-            if i + 2 < NG:
-                vec_a(i + 2)
-            quant("x2", codes_pool, i + 1, E4)
-            quant("di", work, i + 1, E5)
-            quant("dt", codes_pool, i + 1, E5)
-            pe_mm0(i + 1, (0, 1))
-            pe_mm1(i + 1, (0, 1))
+        def gamma_i(i):
+            if i == 0:
+                out = gi[:].rearrange("p (t m j) -> p t m j", t=4, j=J)
+                in_ = sq[:].rearrange("p j (m t) -> p t m j", t=4)
+                nc.scalar.activation(out, in_, ACT.Copy, bias=-PEDESTAL)
 
-        for j in (2, 3):
-            acc_j = psum.tile([P, C], F32, name="tp")
-            acc.append(acc_j)
-        last = NG - 1
-        o1 = keep.tile([P, J, C], F32, name="t", align_bytes=64)
+        def gamma_q(i):
+            if i == 0:
+                nc.vector.quantize_mx(out=gq[:].bitcast(E4), scales=gs[:], in_=gi[:])
 
-        def vec_o1(j):
-            nc.vector.scalar_tensor_tensor(
-                out=o1[:, j, :].rearrange("p (q k) -> p q k", k=J),
-                in0=acc[j][:].rearrange("p (k q) -> p q k", k=J),
-                scalar=2.0,
-                in1=coef[:, j, :].rearrange("p (q k) -> p q k", k=J),
-                op0=ALU.mult, op1=ALU.mult,
-            )
+        def make_coef(i):
+            if i == 0:
+                nc.vector.tensor_scalar(coef[:], gam[:], GAMMA_BOUND, None, op0=ALU.is_gt)
+                nc.vector.tensor_tensor(out=coef[:], in0=coef[:], in1=gam[:], op=ALU.mult)
 
+
+        def load_late(i):
+            if i >= 4:
+                load(i)
+
+        ops = dict(load=load_late, first=act_first, p=vec_p, second=act_second, third=act_third, a=vec_a, t=vec_t, w=vec_w, dn=vec_dn,
+                   turn_x=pe_turn_x, turn_dn=pe_turn_dn, x2=act_x2, dt=act_dt, q_dn=q_dn, q_dt=q_dt, q_x2=q_x2,
+                   mm0a=pe_mm0a, mm0b=pe_mm0b, mm1=pe_mm1, ua=vec_ua, ub=vec_ub, o=vec_o,
+                   gsq=gamma_sq, gi=gamma_i, gq=gamma_q, coef=make_coef)
+        for step in range(-6, NG + 6):
+            for name, ahead in ORDER:
+                i = step + ahead
+                if 0 <= i < NG:
+                    ops[name](i)
+
+        o1 = tpl.tile([P, J, C], F32, name="t", align_bytes=64)
         o1_hbm = out_1.rearrange("(p j) c -> p j c", j=J)
-        add_o(nc.vector, last - 1)
-        store(last - 1)
-        pe_mm0(last, (2, 3))
-        for i in range(NG):
-            pe_mm1(i, (2, 3))
-        vec_u(last, 0)
-        vec_u(last, 1)
-        add_o(nc.gpsimd, last, slice(0, 1))
-        store(last, slice(0, 1))
-        vec_u(last, 2)
-        vec_u(last, 3)
-        add_o(nc.vector, last, slice(1, 4))
-        store(last, slice(1, 4))
-        for half in range(2):
-            vec_o1(2 * half)
-            vec_o1(2 * half + 1)
-            js = slice(2 * half, 2 * half + 2)
+        for js in HALVES:
+            for j in range(js.start, js.stop):
+                nc.vector.scalar_tensor_tensor(
+                    out=o1[:, j, :].rearrange("p (q k) -> p q k", k=J),
+                    in0=coef[:, j, :].rearrange("p (q k) -> p q k", k=J),
+                    scalar=2.0,
+                    in1=acc[j][:].rearrange("p (k q) -> p q k", k=J),
+                    op0=ALU.mult, op1=ALU.mult,
+                )
             nc.sync.dma_start(out=o1_hbm[:, js, :], in_=o1[:, js, :])

@@ -23,7 +23,7 @@ NG = T // G
 GAMMA_BOUND = 2.0 ** (-18)
 PEDESTAL = 2.0 ** (-36)
 FINE = (0,)
-NEWTON = (0,)
+NEWTON = (0, 1)
 DN_BUFS = (4, 2, 2, 5)
 LOADS = ("gam", "n")
 ORDER = (
@@ -158,14 +158,17 @@ def tile_gdn_v_kernel(tc, inputs, beta, gamma, norm, grad_out, out_0, out_1):
 
         def vec_t(i):
             t = get(tpl, "t", i, [P, J, G], F32)
+            factor = 1.5 if i in NEWTON else -0.5
             for js in first_parts(i):
-                nc.vector.tensor_tensor(out=t[:, js, :], in0=st["x", i][:, js, :], in1=st["b", i][:, js, :], op=ALU.mult)
+                nc.vector.scalar_tensor_tensor(out=t[:, js, :], in0=st["x", i][:, js, :], scalar=factor, in1=st["b", i][:, js, :], op0=ALU.mult, op1=ALU.mult)
 
         def vec_dn(i):
             dn = get(dnp, "dn", i, [P, G, J], BF16)
-            nc.vector.scalar_tensor_tensor(
-                out=dn[:], in0=st["n" if i in NEWTON else "a", i][:].rearrange("p j w -> p w j"), scalar=1.5 if i in NEWTON else -0.5,
-                in1=st["t", i][:].rearrange("p j w -> p w j"), op0=ALU.mult, op1=ALU.mult,
+            nc.vector.tensor_tensor(
+                out=dn[:].rearrange("p (c k) j -> p c j k", k=4),
+                in0=st["n" if i in NEWTON else "a", i][:].rearrange("p j (c k) -> p c j k", k=4),
+                in1=st["t", i][:].rearrange("p j (c k) -> p c j k", k=4),
+                op=ALU.mult,
             )
 
         def pe_turn_x(i):

from contextlib import ExitStack

import concourse.mybir as mybir
from concourse.masks import make_identity

B, C, HW = 3, 512, 1024
T = B * HW
FLOPS = 2 * 2 * C * C * T

F32 = mybir.dt.float32
BF16 = mybir.dt.bfloat16
U32 = mybir.dt.uint32
U8 = mybir.dt.uint8
E4 = mybir.dt.float8_e4m3fn_x4
E5 = mybir.dt.float8_e5m2_x4
ALU = mybir.AluOpType
ACT = mybir.ActivationFunctionType

P = 128
J = 4
G = 512
NG = T // G
GAMMA_BOUND = 2.0 ** (-18)
PEDESTAL = 2.0 ** (-36)
FINE = (0,)
NEWTON = (0, 1)
DN_BUFS = (4, 2, 2, 5)
LOADS = ("gam", "n")
ORDER = (
    ("coef", 5),
    ("gsq", 3),
    ("q_dt", -2),
    ("q_dn", 1),
    ("ub", 0),
    ("turn_dn", 0),
    ("a", 2),
    ("mm0a", 1),
    ("load", 4),
    ("gi", 2),
    ("w", 2),
    ("t", 2),
    ("gq", 2),
    ("first", 4),
    ("dt", 0),
    ("mm1", -3),
    ("second", 3),
    ("ua", 1),
    ("turn_x", 0),
    ("o", 0),
    ("third", 3),
    ("mm0b", 1),
    ("x2", 0),
    ("q_x2", -1),
    ("dn", 2),
    ("p", 4),
)


def tile_gdn_v_kernel(tc, inputs, beta, gamma, norm, grad_out, out_0, out_1):
    nc = tc.nc
    x_hbm = inputs.rearrange("b (p j) h w -> b p j (h w)", j=J)
    g_hbm = grad_out.rearrange("b (p j) h w -> b p j (h w)", j=J)
    n_hbm = norm.rearrange("b (p j) h w -> b p j (h w)", j=J)
    o_hbm = out_0.rearrange("b (p j) h w -> b p j (h w)", j=J)

    with ExitStack() as ctx:
        keep = ctx.enter_context(tc.tile_pool(name="keep", bufs=1))
        work = ctx.enter_context(tc.tile_pool(name="work", bufs=2))
        deep = ctx.enter_context(tc.tile_pool(name="deep", bufs=3))
        io = ctx.enter_context(tc.tile_pool(name="io", bufs=DN_BUFS[3]))
        dnp = ctx.enter_context(tc.tile_pool(name="dnp", bufs=DN_BUFS[0]))
        up = ctx.enter_context(tc.tile_pool(name="up", bufs=DN_BUFS[1]))
        tpl = ctx.enter_context(tc.tile_pool(name="tpl", bufs=DN_BUFS[2]))
        whole = ctx.enter_context(tc.tile_pool(name="whole", bufs=NG))
        psum = ctx.enter_context(tc.psum_pool(name="psum", bufs=2))
        accp = ctx.enter_context(tc.psum_pool(name="accp", bufs=1))

        lo, hi = slice(0, 2), slice(2, 4)
        ALLJ = (slice(0, J),)
        HALVES = (lo, hi)

        ident = keep.tile([P, P], F32, name="ident", align_bytes=64)
        warm = keep.tile([P, 8], F32, name="warm")
        nc.vector.memset(warm[:], 1.0)
        nc.scalar.activation(warm[:], warm[:], ACT.Abs_reciprocal_sqrt)

        st = {}

        def tok(i):
            return i // 2, slice((i % 2) * G, (i % 2) * G + G)

        def get(pool, tag, i, shape, dt):
            if (tag, i) not in st:
                new_tile = pool.tile(shape, dt, name=tag, align_bytes=64)
                st[tag, i] = new_tile
            return st[tag, i]

        def first_parts(i):
            return HALVES if i in FINE else ALLJ

        def load_n(i):
            b, w = tok(i)
            n = get(io, "n", i, [P, J, G], F32)
            for js in first_parts(i):
                nc.sync.dma_start(out=n[:, js, :], in_=n_hbm[b, :, js, w])

        def load_g(i):
            b, w = tok(i)
            nc.sync.dma_start(out=get(io, "g", i, [P, J, G], BF16)[:], in_=g_hbm[b, :, :, w])

        def load_x(i):
            b, w = tok(i)
            nc.sync.dma_start(out=get(whole, "x", i, [P, J, G], BF16)[:], in_=x_hbm[b, :, :, w])

        def load(i):
            load_n(i)
            load_g(i)
            load_x(i)

        def act_first(i):
            n, b = st["n", i], get(deep, "b", i, [P, J, G], F32)
            for js in first_parts(i):
                if i in NEWTON:
                    a = get(deep, "a", i, [P, J, G], F32)
                    nc.scalar.activation(b[:, js, :], n[:, js, :], ACT.Abs_reciprocal_sqrt)
                    nc.scalar.activation(a[:, js, :], b[:, js, :], ACT.Square)
                else:
                    nc.scalar.activation(n[:, js, :], n[:, js, :], ACT.Square)
                    nc.scalar.activation(b[:, js, :], n[:, js, :], ACT.Abs_reciprocal_sqrt)

        def vec_p(i):
            n = st["n", i]
            for js in first_parts(i):
                nc.vector.tensor_tensor(out=n[:, js, :], in0=n[:, js, :], in1=st["a" if i in NEWTON else "b", i][:, js, :], op=ALU.mult)

        def act_second(i):
            n = st["n", i]
            for js in () if i in NEWTON else first_parts(i):
                nc.scalar.activation(n[:, js, :], n[:, js, :], ACT.Square)
                nc.scalar.activation(n[:, js, :], n[:, js, :], ACT.Abs_reciprocal_sqrt)

        def vec_w(i):
            n = st["n", i]
            for js in first_parts(i) if i in NEWTON else ():
                nc.vector.scalar_tensor_tensor(out=n[:, js, :], in0=n[:, js, :], scalar=4.0 / 3.0, in1=st["a", i][:, js, :], op0=ALU.subtract, op1=ALU.mult)

        def act_third(i):
            n, b = st["n", i], st["b", i]
            for js in first_parts(i):
                r = st["a", i] if i in NEWTON else n
                nc.scalar.activation(b[:, js, :], r[:, js, :], ACT.Square)

        def vec_a(i):
            a = get(deep, "a", i, [P, J, G], F32)
            r = a if i in NEWTON else st["n", i]
            for js in first_parts(i):
                nc.vector.tensor_tensor(out=a[:, js, :], in0=st["g", i][:, js, :], in1=r[:, js, :], op=ALU.mult)

        def vec_t(i):
            t = get(tpl, "t", i, [P, J, G], F32)
            factor = 1.5 if i in NEWTON else -0.5
            for js in first_parts(i):
                nc.vector.scalar_tensor_tensor(out=t[:, js, :], in0=st["x", i][:, js, :], scalar=factor, in1=st["b", i][:, js, :], op0=ALU.mult, op1=ALU.mult)

        def vec_dn(i):
            dn = get(dnp, "dn", i, [P, G, J], BF16)
            nc.vector.tensor_tensor(
                out=dn[:].rearrange("p (c k) j -> p c j k", k=4),
                in0=st["n" if i in NEWTON else "a", i][:].rearrange("p j (c k) -> p c j k", k=4),
                in1=st["t", i][:].rearrange("p j (c k) -> p c j k", k=4),
                op=ALU.mult,
            )

        def pe_turn_x(i):
            words = st["x", i][:].rearrange("p j w -> p (j w)").bitcast(F32)
            for hb in range(2):
                tp = psum.tile([P, 2, 2 * P], F32, name="tp")
                st["xt", i, hb] = tp
                for u in range(2):
                    for jj in range(2):
                        j = 2 * hb + jj
                        nc.tensor.transpose(tp[:, u, jj * P : jj * P + P], words[:, j * (G // 2) + u : (j + 1) * (G // 2) : 2], ident[:])

        def pe_turn_dn(i):
            words = st["dn", i][:].rearrange("p w j -> p (w j)").bitcast(F32)
            for hb in range(2):
                tp = psum.tile([P, J, P], F32, name="tp")
                st["dt", i, hb] = tp
                for t in range(4):
                    nc.tensor.transpose(tp[:, t, :], words[:, 2 * t + hb : 2 * G : 8], ident[:])

        def act_x2(i):
            x2 = get(work, "x2", i, [P, 4 * C], BF16)
            for hb in range(2):
                tp = st["xt", i, hb]
                nc.scalar.activation(
                    x2[:, 1024 * hb : 1024 * hb + 1024].rearrange("q (c u e) -> q c u e", u=2, e=2),
                    tp[:].rearrange("q u c -> q (u c)").bitcast(BF16).rearrange("q (u c e) -> q c u e", u=2, e=2),
                    ACT.Square,
                )

        def act_dt(i):
            dt = get(work, "dtt", i, [P, 4 * C], BF16)
            for hb in range(2):
                nc.scalar.copy(
                    dt[:, 1024 * hb : 1024 * hb + 1024].rearrange("q (b m t) -> q b m t", b=2, t=4),
                    st["dt", i, hb][:].rearrange("q t m -> q (t m)").bitcast(BF16).rearrange("q (t m b) -> q b m t", t=4, b=2),
                )

        def quant(key, pool, i, dt):
            codes = get(pool, key + "q", i, [P, G], U32)
            scales = get(pool, key + "s", i, [P, G], U8)
            src = st[key, i][:]
            if key == "dn":
                src = src.rearrange("p w j -> p (w j)")
            nc.vector.quantize_mx(out=codes[:].bitcast(dt), scales=scales[:], in_=src)

        def q_dn(i):
            quant("dn", work, i, E5)

        def q_dt(i):
            quant("dtt", work, i, E5)

        def q_x2(i):
            quant("x2", work, i, E4)

        def pe_mm0(i, tiles):
            for t in tiles:
                pp = psum.tile([P, G], F32, name="pp")
                st["pp", i, t] = pp
                cols = slice(P * t, P * t + P)
                nc.tensor.matmul_mx(
                    out=pp[:], lhsT=gq[:, cols].bitcast(E4), lhsT_scale=gs[:, cols],
                    rhs=st["dnq", i][:].bitcast(E5), rhs_scale=st["dns", i][:], start=True, stop=True,
                )

        def pe_mm0a(i):
            pe_mm0(i, (0, 1))

        def pe_mm0b(i):
            pe_mm0(i, (2, 3))

        def pe_mm1(i):
            for j in range(J):
                cols = slice(P * j, P * j + P)
                nc.tensor.matmul_mx(
                    out=acc[j][:], lhsT=st["dttq", i][:, cols].bitcast(E5), lhsT_scale=st["dtts", i][:, cols],
                    rhs=st["x2q", i][:].bitcast(E4), rhs_scale=st["x2s", i][:], start=(i == 0), stop=(i == NG - 1),
                )

        def vec_u(i, tiles):
            u = get(up, "u", i, [P, J, G], F32)
            for t in tiles:
                nc.vector.scalar_tensor_tensor(out=u[:, t, :], in0=st["x", i][:, t, :], scalar=2.0, in1=st["pp", i, t][:], op0=ALU.mult, op1=ALU.mult)

        def vec_ua(i):
            vec_u(i, (0, 1))

        def vec_ub(i):
            vec_u(i, (2, 3))

        def vec_o(i):
            b, w = tok(i)
            u = st["u", i]
            for js in HALVES if i == NG - 1 else ALLJ:
                nc.vector.tensor_tensor(out=u[:, js, :], in0=u[:, js, :], in1=st["a", i][:, js, :], op=ALU.add)
                nc.sync.dma_start(out=o_hbm[b, :, js, w], in_=u[:, js, :])

        acc = []
        for j in range(J):
            acc_j = accp.tile([P, C], F32, name="acc%d" % j)
            acc.append(acc_j)

        gam = keep.tile([P, J, C], BF16, name="gam", align_bytes=64)
        for what in LOADS:
            if what == "gam":
                nc.sync.dma_start(out=gam[:], in_=gamma.rearrange("(p j) c -> p j c", j=J))
            if what == "n":
                load_n(0)
        load_g(0)
        load_x(0)
        for i in range(1, 4):
            load(i)
        make_identity(nc, ident[:])

        gm = work.tile([P, J, C], BF16, name="x2", align_bytes=64)
        nc.vector.tensor_scalar_max(gm[:], gam[:], GAMMA_BOUND)
        sq = deep.tile([P, J, G], F32, name="b", align_bytes=64)
        gi = work.tile([P, C * J], BF16, name="dtt", align_bytes=64)
        gq = keep.tile([P, C], U32, name="gq", align_bytes=64)
        gs = keep.tile([P, C], U8, name="gs", align_bytes=64)
        coef = keep.tile([P, J, C], BF16, name="coef", align_bytes=64)

        def gamma_sq(i):
            if i == 0:
                nc.scalar.activation(sq[:], gm[:], ACT.Square)

        def gamma_i(i):
            if i == 0:
                out = gi[:].rearrange("p (t m j) -> p t m j", t=4, j=J)
                in_ = sq[:].rearrange("p j (m t) -> p t m j", t=4)
                nc.scalar.activation(out, in_, ACT.Copy, bias=-PEDESTAL)

        def gamma_q(i):
            if i == 0:
                nc.vector.quantize_mx(out=gq[:].bitcast(E4), scales=gs[:], in_=gi[:])

        def make_coef(i):
            if i == 0:
                nc.vector.tensor_scalar(coef[:], gam[:], GAMMA_BOUND, None, op0=ALU.is_gt)
                nc.vector.tensor_tensor(out=coef[:], in0=coef[:], in1=gam[:], op=ALU.mult)


        def load_late(i):
            if i >= 4:
                load(i)

        ops = dict(load=load_late, first=act_first, p=vec_p, second=act_second, third=act_third, a=vec_a, t=vec_t, w=vec_w, dn=vec_dn,
                   turn_x=pe_turn_x, turn_dn=pe_turn_dn, x2=act_x2, dt=act_dt, q_dn=q_dn, q_dt=q_dt, q_x2=q_x2,
                   mm0a=pe_mm0a, mm0b=pe_mm0b, mm1=pe_mm1, ua=vec_ua, ub=vec_ub, o=vec_o,
                   gsq=gamma_sq, gi=gamma_i, gq=gamma_q, coef=make_coef)
        for step in range(-6, NG + 6):
            for name, ahead in ORDER:
                i = step + ahead
                if 0 <= i < NG:
                    ops[name](i)

        o1 = tpl.tile([P, J, C], F32, name="t", align_bytes=64)
        o1_hbm = out_1.rearrange("(p j) c -> p j c", j=J)
        for js in HALVES:
            for j in range(js.start, js.stop):
                nc.vector.scalar_tensor_tensor(
                    out=o1[:, j, :].rearrange("p (q k) -> p q k", k=J),
                    in0=coef[:, j, :].rearrange("p (q k) -> p q k", k=J),
                    scalar=2.0,
                    in1=acc[j][:].rearrange("p (k q) -> p q k", k=J),
                    op0=ALU.mult, op1=ALU.mult,
                )
            nc.sync.dma_start(out=o1_hbm[:, js, :], in_=o1[:, js, :])
